import numpy as np
import ml_dtypes


def mxq(x, axis, fmt="e4m3"):
    dtype, down = {"e4m3": (ml_dtypes.float8_e4m3fn, 7), "e5m2": (ml_dtypes.float8_e5m2, 14)}[fmt]
    v = np.moveaxis(np.asarray(x, np.float32).astype(ml_dtypes.bfloat16).astype(np.float64), axis, -1)
    blocks = v.reshape(v.shape[:-1] + (-1, 32))
    amax = np.abs(blocks).max(-1, keepdims=True)
    byte = np.maximum(np.where(amax > 0, np.frexp(amax)[1] - 1 + 127, 0) - down, 1)
    scale = np.exp2(byte - 127.0)
    codes = (blocks / scale).astype(np.float32).astype(dtype).astype(np.float64)
    return np.moveaxis((codes * scale).reshape(v.shape), -1, axis)


WIDE = False


def mx_kscale(k):
    if not WIDE:
        return np.ones(k)
    levels = np.array([10, -10, 5, -5, 0])
    if k % 512:
        return np.exp2(np.random.permutation(np.resize(levels, k // 32))).repeat(32)
    a = np.empty((k // 512, 16))
    for p in range(k // 512):
        a[p, :8] = np.random.permutation(np.resize(levels, 8))
        for g in range(8):
            far = levels[np.abs(levels - a[p, g]) >= 10]
            a[p, g + 8] = far[np.random.randint(len(far))]
    return np.exp2(a.ravel()).repeat(32)


BF16 = ml_dtypes.bfloat16


def bf(x):
    return np.asarray(x, np.float32).astype(BF16)


def f64(x):
    return np.asarray(x).astype(np.float64)


B, N, C, D = 2, 2048, 2048, 2048
ETA, TAU = 1.0, 1.5


def setup_inputs():
    s, t = mx_kscale(C), mx_kscale(D)
    a = 2.0 * (C / D) ** 0.25 / np.sqrt(C)
    return {"H_t": bf(np.random.standard_normal((B, N, C)) * s),
            "A_stat": bf(np.random.random((N, N))),
            "M_mask": bf(np.random.random((N, N)) - 0.25),
            "Wq": bf(np.random.standard_normal((D, C)) * a * t[:, None] / s),
            "Wk": bf(np.random.standard_normal((D, C)) * a / t[:, None] / s)}


def reference(H_t, A_stat, M_mask, Wq, Wk):
    c = H_t.shape[-1]
    hq = mxq(f64(H_t), 2, "e4m3")
    Q = hq @ mxq(f64(Wq), 1, "e4m3").T
    K = hq @ mxq(f64(Wk), 1, "e4m3").T
    logits = (mxq(Q, 2, "e4m3") @ mxq(K, 2, "e4m3").transpose(0, 2, 1)) / (np.sqrt(c) * TAU)
    logits = 0.5 * (logits + logits.transpose(0, 2, 1))
    n = logits.shape[-1]
    eye = np.eye(n, dtype=bool)
    logits = np.where(eye[None, :, :], -np.inf, logits)
    A_bias = np.where(eye, 0.0, f64(A_stat))
    logits = logits + ETA * A_bias[None, :, :]
    logits = np.where((f64(M_mask) <= 0)[None, :, :], -np.inf, logits)
    e = np.exp(logits - logits.max(-1, keepdims=True))
    return e / e.sum(-1, keepdims=True)

@@ -1,0 +1,321 @@
+from contextlib import ExitStack
+import math
+
+import concourse.mybir as mybir
+from concourse.masks import make_identity
+
+F32 = mybir.dt.float32
+BF16 = mybir.dt.bfloat16
+U32 = mybir.dt.uint32
+U8 = mybir.dt.uint8
+FP8X4 = mybir.dt.float8_e4m3fn_x4
+ACT = mybir.ActivationFunctionType
+ALU = mybir.AluOpType
+AX = mybir.AxisListType
+
+P = 128
+NT = 2048
+KD = 2048
+CH = 512
+NPASS = KD // CH
+NCH = NT // CH
+NRB = NT // P
+FLOPS = 3 * 2 * 2 * 2048 * 2048 * 2048
+LOGIT_SCALE = 0.5 / (math.sqrt(2048.0) * 1.5)
+NEG_BIG = -1.0e30
+
+BUFS = {
+    "ident": 1, "dneg": 1, "warm": 1,
+    "big": 24, "pl": 24,
+    "hraw": 2, "gin": 3, "g2": 2, "tmp": 2,
+    "mx": 3, "nmx": 3, "sm": 3, "rs": 3,
+}
+W_IN_FLIGHT = 5
+
+
+def tile_dynamicgraphattention_l_kernel(tc, H_t, A_stat, M_mask, Wq, Wk, out):
+    nc = tc.nc
+    with ExitStack() as ctx:
+        sb = ctx.enter_context(tc.tile_pool(name="sb", bufs=1))
+        ps = ctx.enter_context(tc.psum_pool(name="ps", bufs=4))
+        ctx.enter_context(tc.manual_schedule())
+
+        def sbt(shape, dtype, tag):
+            return sb.tile(shape, dtype, name="t_%s" % tag, tag=tag, bufs=BUFS[tag], align_bytes=64)
+
+        def pst(shape, tag):
+            return ps.tile(shape, F32, name="p_%s" % tag, tag=tag, bufs=4)
+
+        wsrc = (Wq, Wk)
+        wc = {}
+        wp = {}
+        hc = {}
+        hp = {}
+        qk = {}
+        qkp = {}
+        raw = {}
+        rt = {}
+        amt = {}
+        pend_load = {"w": [], "h": []}
+        pendq = []
+        later = []
+        rfree = []
+
+        ident = sbt([P, P], F32, "ident")
+        make_identity(nc, ident[:])
+        dneg = sbt([P, P], BF16, "dneg")
+        nc.vector.tensor_scalar_mul(out=dneg[:], in0=ident[:], scalar1=NEG_BIG)
+        warm = sbt([P, 2], F32, "warm")
+        nc.vector.memset(warm[:, 0:1], 0.0)
+        nc.scalar.activation(out=warm[:, 1:2], in_=warm[:, 0:1], func=ACT.Exp)
+
+        def tick():
+            if later:
+                later.pop(0)()
+
+        def load_block(key):
+            if key[0] == "h":
+                row0 = CH * key[2] + P * key[3]
+                src = H_t[key[1], row0:row0 + P, :]
+            else:
+                grp = wsrc[key[1]][CH * key[2]:CH * (key[2] + 1), :]
+                src = grp.rearrange("(m t) k -> m t k", t=4)[:, key[3], :]
+            early = key[0] == "w" or (key[1] == 0 and key[2] == 0)
+            t = sbt([P, KD], BF16, "big" if early else "hraw")
+            nc.sync.dma_start(out=t[:], in_=src)
+            raw[key] = t
+
+        def block_dest(key):
+            kk = (key[1], key[2])
+            cd, pl = (hc, hp) if key[0] == "h" else (wc, wp)
+            if kk not in cd:
+                cd[kk] = sbt([P, NPASS, CH], U32, "big")
+                pl[kk] = sbt([P, CH], U8, "pl")
+            return cd[kk], pl[kk]
+
+        def quant_bank(item):
+            key, h, gin = item
+            codes, planes = block_dest(key)
+            col = P * key[3]
+            for g2 in range(2):
+                g = 2 * h + g2
+                nc.vector.quantize_mx(
+                    out=codes[:, g, col:col + P].bitcast(FP8X4),
+                    scales=planes[4 * g:P, col:col + P],
+                    in_=gin[:, g2].rearrange("p r j -> p (r j)"),
+                )
+
+        def do_run(keys):
+            banks = []
+            for key in keys:
+                words = raw[key][:].bitcast(F32)
+                for h in range(2):
+                    xt = pst([P, 2, 2, P], "tp")
+                    for g2 in range(2):
+                        g = 2 * h + g2
+                        for u in range(2):
+                            nc.tensor.transpose(xt[:, g2, u, :], words[:, 256 * g + u:256 * (g + 1):2], ident[:])
+                    banks.append((key, h, xt))
+                q = pend_load[key[0]]
+                if q and key[0:3] != ("h", 0, 0):
+                    load_block(q.pop(0))
+            gins = []
+            for n in range(len(banks)):
+                key, h, xt = banks[n]
+                if n == 3:
+                    quant_bank(gins[0])
+                gin = sbt([P, 2, P, 4], BF16, "gin")
+                src = xt[:].rearrange("p g u r -> p g r u")
+                if n % 2 == 0:
+                    nc.scalar.copy(out=gin[:].bitcast(F32), in_=src)
+                else:
+                    nc.vector.tensor_copy(out=gin[:].bitcast(F32), in_=src)
+                gins.append((key, h, gin))
+            for n in range(1, len(gins)):
+                quant_bank(gins[n])
+
+        def run_thunk(keys):
+            def f():
+                do_run(keys)
+            return f
+
+        def hruns(b, c):
+            return [[("h", b, c, 0), ("h", b, c, 1)], [("h", b, c, 2), ("h", b, c, 3)]]
+
+        def wruns(w, G):
+            return [[("w", w, G, 0), ("w", w, G, 1)], [("w", w, G, 2), ("w", w, G, 3)]]
+
+        def flush_q():
+            while pendq:
+                g2t, kk, G = pendq.pop(0)
+                if kk not in qk:
+                    qk[kk] = sbt([P, NPASS, CH], U32, "big")
+                    qkp[kk] = sbt([P, CH], U8, "pl")
+                nc.vector.quantize_mx(
+                    out=qk[kk][:, G, :].bitcast(FP8X4),
+                    scales=qkp[kk][4 * G:P, :],
+                    in_=g2t[:].rearrange("p n t -> p (n t)"),
+                )
+
+        def unit(b, c, w, G, slots):
+            tmp = sbt([P, 4, CH], BF16, "tmp")
+            for t in range(4):
+                if t % 2 == 0 and slots:
+                    slots.pop(0)()
+                acc = pst([P, CH], "acc")
+                for g in range(NPASS):
+                    nc.tensor.matmul_mx(
+                        out=acc[:],
+                        lhsT=wc[(w, G)][:, g, P * t:P * (t + 1)].bitcast(FP8X4),
+                        lhsT_scale=wp[(w, G)][4 * g:P, P * t:P * (t + 1)],
+                        rhs=hc[(b, c)][:, g, :].bitcast(FP8X4),
+                        rhs_scale=hp[(b, c)][4 * g:P, :],
+                        start=(g == 0),
+                        stop=(g == NPASS - 1),
+                    )
+                nc.scalar.copy(out=tmp[:, t, :], in_=acc[:])
+            g2t = sbt([P, CH, 4], BF16, "g2")
+            nc.vector.tensor_copy(out=g2t[:], in_=tmp[:].rearrange("p t n -> p n t"))
+            flush_q()
+            pendq.append((g2t, (b, w, c), G))
+
+        def load_am(i):
+            a = sbt([P, NT], BF16, "hraw" if i == 0 else "g2")
+            nc.sync.dma_start(out=a[:], in_=A_stat[P * i:P * (i + 1), :])
+            m = sbt([P, NT], BF16, "hraw" if i == 0 else "tmp")
+            nc.sync.dma_start(out=m[:], in_=M_mask[P * i:P * (i + 1), :])
+            amt[i] = (a, m)
+
+        def bias(i):
+            a, m = amt[i]
+            nc.vector.tensor_scalar(out=m[:], in0=m[:], scalar1=0.0, scalar2=NEG_BIG, op0=ALU.is_le, op1=ALU.mult)
+            dg = a[:, P * i:P * (i + 1)]
+            nc.vector.tensor_tensor(out=dg, in0=dg, in1=dneg[:], op=ALU.add)
+            nc.vector.tensor_tensor(out=a[:], in0=a[:], in1=m[:], op=ALU.add)
+
+        def exp_thunk(srow, nmx, sm):
+            def f():
+                nc.scalar.activation(out=srow[:], in_=srow[:], func=ACT.Exp, bias=nmx[:], scale=1.0, accum_out=sm[:])
+            return f
+
+        def norm_thunk(b, i, srow, sm):
+            def f():
+                rs = sbt([P, 1], F32, "rs")
+                nc.vector.reciprocal(out=rs[:], in_=sm[:])
+                nc.scalar.activation(out=srow[:], in_=srow[:], func=ACT.Copy, scale=rs[:])
+                nc.scalar.dma_start(out=out[b, P * i:P * (i + 1), :], in_=srow[:])
+            return f
+
+        def r_block():
+            if not rfree:
+                page = sbt([P, 16, P], F32, "big")
+                for n in range(16):
+                    rfree.append(page[:, n, :])
+            return rfree.pop(0)
+
+        def row_step(b, i):
+            if b == 0 and i + 1 < NRB:
+                load_am(i + 1)
+            tick()
+            bm = amt[i][0]
+            srow = sbt([P, NT], F32, "big")
+            tps = []
+            for q in range((i + 3) // 4):
+                nblk = min(4, i - 4 * q)
+                xt = pst([P, 4, P], "tp")
+                for jj in range(nblk):
+                    blk = rt.pop((b, 4 * q + jj, i))
+                    nc.tensor.transpose(xt[:, jj, :], blk, ident[:])
+                    rfree.append(blk)
+                tps.append((q, nblk, xt))
+            for q, nblk, xt in tps:
+                nc.vector.tensor_tensor(
+                    out=srow[:, CH * q:CH * q + P * nblk],
+                    in0=xt[:, 0:nblk, :].rearrange("p j c -> p (j c)"),
+                    in1=bm[:, CH * q:CH * q + P * nblk],
+                    op=ALU.add,
+                )
+            ci, r = divmod(i, 4)
+            for cj in range(ci, NCH):
+                lo = r if cj == ci else 0
+                groups = {0: [(0, 4)], 1: [(1, 1), (2, 2)], 2: [(2, 2)], 3: [(3, 1)]}[lo]
+                acc = pst([P, CH], "acc")
+                for b0, nb in groups:
+                    o0 = (b0 - lo) * P
+                    n = 0
+                    for G in range(NPASS):
+                        for sa in range(2):
+                            st = (b, sa, ci)
+                            mv = (b, 1 - sa, cj)
+                            nc.tensor.matmul_mx(
+                                out=acc[:, o0:o0 + P * nb],
+                                lhsT=qk[st][:, G, P * r:P * (r + 1)].bitcast(FP8X4),
+                                lhsT_scale=qkp[st][4 * G:P, P * r:P * (r + 1)],
+                                rhs=qk[mv][:, G, P * b0:P * (b0 + nb)].bitcast(FP8X4),
+                                rhs_scale=qkp[mv][4 * G:P, P * b0:P * (b0 + nb)],
+                                start=(n == 0),
+                                stop=(n == 2 * NPASS - 1),
+                            )
+                            n += 1
+                wcols = (4 - lo) * P
+                col0 = CH * cj + P * lo
+                nc.vector.scalar_tensor_tensor(
+                    out=srow[:, col0:col0 + wcols], in0=acc[:, 0:wcols], scalar=LOGIT_SCALE,
+                    in1=bm[:, col0:col0 + wcols], op0=ALU.mult, op1=ALU.add,
+                )
+                for blk in range(lo, 4):
+                    j = 4 * cj + blk
+                    if j > i:
+                        rtile = r_block()
+                        nc.scalar.activation(
+                            out=rtile, in_=acc[:, (blk - lo) * P:(blk - lo + 1) * P], func=ACT.Copy, scale=LOGIT_SCALE
+                        )
+                        rt[(b, i, j)] = rtile
+                if cj == ci:
+                    tick()
+            mx = sbt([P, 1], F32, "mx")
+            nc.vector.reduce_max(out=mx[:], in_=srow[:], axis=AX.X)
+            nmx = sbt([P, 1], F32, "nmx")
+            nc.vector.tensor_scalar_mul(out=nmx[:], in0=mx[:], scalar1=-1.0)
+            if b == 1 and i + 1 < NRB:
+                bias(i + 1)
+            sm = sbt([P, 1], F32, "sm")
+            later.append(exp_thunk(srow, nmx, sm))
+            later.append(norm_thunk(b, i, srow, sm))
+
+        units = [(w, G) for w in range(2) for G in range(NPASS)]
+        wblocks = [("w", w, G, t) for w, G in units for t in range(4)]
+        head = [("h", 0, 0, 0), ("h", 0, 0, 1), wblocks[0], wblocks[1], ("h", 0, 0, 2), ("h", 0, 0, 3)] + wblocks[2:W_IN_FLIGHT]
+        for key in head:
+            load_block(key)
+        pend_load["w"].extend(wblocks[W_IN_FLIGHT:])
+        hq = [("h", m // NCH, m % NCH, r) for m in range(1, 2 * NCH) for r in range(4)]
+        load_block(hq[0])
+        load_block(hq[1])
+        pend_load["h"].extend(hq[2:])
+
+        do_run(hruns(0, 0)[0][0:2])
+        do_run(wruns(0, 0)[0])
+        do_run(hruns(0, 0)[1])
+        do_run(wruns(0, 0)[1])
+
+        for m in range(2 * NCH):
+            for ui in range(8):
+                w, G = units[ui]
+                slots = []
+                if m == 0 and ui < 7:
+                    slots = [run_thunk(k) for k in wruns(units[ui + 1][0], units[ui + 1][1])]
+                elif m + 1 < 2 * NCH and ((m == 0 and ui == 7) or (m > 0 and ui == 4)):
+                    slots = [run_thunk(k) for k in hruns((m + 1) // NCH, (m + 1) % NCH)]
+                unit(m // NCH, m % NCH, w, G, slots)
+                if m == 2 * NCH - 1 and ui == 3:
+                    load_am(0)
+                if m == 2 * NCH - 1 and ui == 6:
+                    bias(0)
+        flush_q()
+
+        for i in range(NRB):
+            for b in range(2):
+                row_step(b, i)
+        while later:
+            tick()

@@ -31,6 +31,10 @@ BUFS = {
     "mx": 3, "nmx": 3, "sm": 3, "rs": 3,
 }
 W_IN_FLIGHT = 5
+SORT_H = True
+SORT_W = 0
+G_ADD = True
+G_NORM_FROM = 6
 
 
 def tile_dynamicgraphattention_l_kernel(tc, H_t, A_stat, M_mask, Wq, Wk, out):
@@ -54,6 +58,7 @@ def tile_dynamicgraphattention_l_kernel(tc, H_t, A_stat, M_mask, Wq, Wk, out):
         qk = {}
         qkp = {}
         raw = {}
+        srt = {}
         rt = {}
         amt = {}
         pend_load = {"w": [], "h": []}
@@ -85,6 +90,17 @@ def tile_dynamicgraphattention_l_kernel(tc, H_t, A_stat, M_mask, Wq, Wk, out):
             nc.sync.dma_start(out=t[:], in_=src)
             raw[key] = t
 
+        def next_load(key):
+            q = pend_load[key[0]]
+            if q and key[0:3] != ("h", 0, 0):
+                load_block(q.pop(0))
+
+        def sort_block(key):
+            s = sbt([P, NPASS, 2, P], F32, "big")
+            nc.scalar.copy(out=s[:], in_=raw[key][:].bitcast(F32).rearrange("r (g p u) -> r g u p", g=NPASS, u=2))
+            srt[key] = s
+            next_load(key)
+
         def block_dest(key):
             kk = (key[1], key[2])
             cd, pl = (hc, hp) if key[0] == "h" else (wc, wp)
@@ -114,11 +130,13 @@ def tile_dynamicgraphattention_l_kernel(tc, H_t, A_stat, M_mask, Wq, Wk, out):
                     for g2 in range(2):
                         g = 2 * h + g2
                         for u in range(2):
-                            nc.tensor.transpose(xt[:, g2, u, :], words[:, 256 * g + u:256 * (g + 1):2], ident[:])
+                            if key in srt:
+                                nc.tensor.transpose(xt[:, g2, u, :], srt[key][:, g, u, :], ident[:])
+                            else:
+                                nc.tensor.transpose(xt[:, g2, u, :], words[:, 256 * g + u:256 * (g + 1):2], ident[:])
                     banks.append((key, h, xt))
-                q = pend_load[key[0]]
-                if q and key[0:3] != ("h", 0, 0):
-                    load_block(q.pop(0))
+                if key not in srt:
+                    next_load(key)
             gins = []
             for n in range(len(banks)):
                 key, h, xt = banks[n]
@@ -180,7 +198,7 @@ def tile_dynamicgraphattention_l_kernel(tc, H_t, A_stat, M_mask, Wq, Wk, out):
             pendq.append((g2t, (b, w, c), G))
 
         def load_am(i):
-            a = sbt([P, NT], BF16, "hraw" if i == 0 else "g2")
+            a = sbt([P, NT], BF16, "hraw" if i % 2 == 0 else "g2")
             nc.sync.dma_start(out=a[:], in_=A_stat[P * i:P * (i + 1), :])
             m = sbt([P, NT], BF16, "hraw" if i == 0 else "tmp")
             nc.sync.dma_start(out=m[:], in_=M_mask[P * i:P * (i + 1), :])
@@ -191,7 +209,10 @@ def tile_dynamicgraphattention_l_kernel(tc, H_t, A_stat, M_mask, Wq, Wk, out):
             nc.vector.tensor_scalar(out=m[:], in0=m[:], scalar1=0.0, scalar2=NEG_BIG, op0=ALU.is_le, op1=ALU.mult)
             dg = a[:, P * i:P * (i + 1)]
             nc.vector.tensor_tensor(out=dg, in0=dg, in1=dneg[:], op=ALU.add)
-            nc.vector.tensor_tensor(out=a[:], in0=a[:], in1=m[:], op=ALU.add)
+            if G_ADD:
+                nc.gpsimd.tensor_tensor(out=a[:], in0=a[:], in1=m[:], op=ALU.add)
+            else:
+                nc.vector.tensor_tensor(out=a[:], in0=a[:], in1=m[:], op=ALU.add)
 
         def exp_thunk(srow, nmx, sm):
             def f():
@@ -202,8 +223,12 @@ def tile_dynamicgraphattention_l_kernel(tc, H_t, A_stat, M_mask, Wq, Wk, out):
             def f():
                 rs = sbt([P, 1], F32, "rs")
                 nc.vector.reciprocal(out=rs[:], in_=sm[:])
-                nc.scalar.activation(out=srow[:], in_=srow[:], func=ACT.Copy, scale=rs[:])
-                nc.scalar.dma_start(out=out[b, P * i:P * (i + 1), :], in_=srow[:])
+                if b == 1 and i >= G_NORM_FROM:
+                    nc.gpsimd.tensor_scalar(out=srow[:], in0=srow[:], scalar1=rs[:], scalar2=0.0, op0=ALU.mult, op1=ALU.add)
+                    nc.sync.dma_start(out=out[b, P * i:P * (i + 1), :], in_=srow[:])
+                else:
+                    nc.scalar.activation(out=srow[:], in_=srow[:], func=ACT.Copy, scale=rs[:])
+                    nc.scalar.dma_start(out=out[b, P * i:P * (i + 1), :], in_=srow[:])
             return f
 
         def r_block():
@@ -214,8 +239,8 @@ def tile_dynamicgraphattention_l_kernel(tc, H_t, A_stat, M_mask, Wq, Wk, out):
             return rfree.pop(0)
 
         def row_step(b, i):
-            if b == 0 and i + 1 < NRB:
-                load_am(i + 1)
+            if b == 1 and i + 2 < NRB:
+                load_am(i + 2)
             tick()
             bm = amt[i][0]
             srow = sbt([P, NT], F32, "big")
@@ -277,7 +302,7 @@ def tile_dynamicgraphattention_l_kernel(tc, H_t, A_stat, M_mask, Wq, Wk, out):
             nc.vector.reduce_max(out=mx[:], in_=srow[:], axis=AX.X)
             nmx = sbt([P, 1], F32, "nmx")
             nc.vector.tensor_scalar_mul(out=nmx[:], in0=mx[:], scalar1=-1.0)
-            if b == 1 and i + 1 < NRB:
+            if b == (0 if G_ADD else 1) and i + 1 < NRB:
                 bias(i + 1)
             sm = sbt([P, 1], F32, "sm")
             later.append(exp_thunk(srow, nmx, sm))
@@ -300,19 +325,35 @@ def tile_dynamicgraphattention_l_kernel(tc, H_t, A_stat, M_mask, Wq, Wk, out):
         do_run(wruns(0, 0)[1])
 
         for m in range(2 * NCH):
+            nruns = hruns((m + 1) // NCH, (m + 1) % NCH) if m + 1 < 2 * NCH else []
+            do_sort = SORT_H and m < 2 * NCH - 2
             for ui in range(8):
                 w, G = units[ui]
                 slots = []
                 if m == 0 and ui < 7:
                     slots = [run_thunk(k) for k in wruns(units[ui + 1][0], units[ui + 1][1])]
-                elif m + 1 < 2 * NCH and ((m == 0 and ui == 7) or (m > 0 and ui == 4)):
-                    slots = [run_thunk(k) for k in hruns((m + 1) // NCH, (m + 1) % NCH)]
+                elif nruns and m == 0 and ui == 7:
+                    slots = [run_thunk(k) for k in nruns]
+                elif nruns and m > 0 and ui == 4:
+                    slots = [run_thunk(nruns[0])]
+                elif nruns and m > 0 and ui == 6:
+                    slots = [run_thunk(nruns[1])]
                 unit(m // NCH, m % NCH, w, G, slots)
+                if do_sort and ui == (5 if m == 0 else 2):
+                    sort_block(nruns[0][0])
+                    sort_block(nruns[0][1])
+                if do_sort and ui == (6 if m == 0 else 4):
+                    sort_block(nruns[1][0])
+                    sort_block(nruns[1][1])
+                if m == 0 and ui < 6 and SORT_W:
+                    for k in wruns(units[ui + 2][0], units[ui + 2][1])[0][0:SORT_W]:
+                        sort_block(k)
                 if m == 2 * NCH - 1 and ui == 3:
                     load_am(0)
                 if m == 2 * NCH - 1 and ui == 6:
                     bias(0)
         flush_q()
+        load_am(1)
 
         for i in range(NRB):
             for b in range(2):

@@ -22,19 +22,22 @@ NCH = NT // CH
 NRB = NT // P
 FLOPS = 3 * 2 * 2 * 2048 * 2048 * 2048
 LOGIT_SCALE = 0.5 / (math.sqrt(2048.0) * 1.5)
-NEG_BIG = -1.0e30
+BIG = 1.0e30
 
 BUFS = {
     "ident": 1, "dneg": 1, "warm": 1,
     "big": 24, "pl": 24,
     "hraw": 2, "gin": 3, "g2": 2, "tmp": 2,
-    "mx": 3, "nmx": 3, "sm": 3, "rs": 3,
+    "nmx": 3, "sm": 3, "rs": 3,
 }
-W_IN_FLIGHT = 5
-SORT_H = True
-SORT_W = 0
+LEAD = (7, 3)
+SORT_LEAD = 3
+SORT_FROM = 3
+N_EARLY = 28
+E_IN_FLIGHT = 8
 G_ADD = True
 G_NORM_FROM = 6
+MERGE_TP_UPTO = 8
 
 
 def tile_dynamicgraphattention_l_kernel(tc, H_t, A_stat, M_mask, Wq, Wk, out):
@@ -61,15 +64,19 @@ def tile_dynamicgraphattention_l_kernel(tc, H_t, A_stat, M_mask, Wq, Wk, out):
         srt = {}
         rt = {}
         amt = {}
-        pend_load = {"w": [], "h": []}
+        pend_load = {"e": [], "l": []}
+        early = set()
+        run_at = {}
+        sort_at = {}
         pendq = []
         later = []
         rfree = []
+        tps = {}
 
         ident = sbt([P, P], F32, "ident")
         make_identity(nc, ident[:])
         dneg = sbt([P, P], BF16, "dneg")
-        nc.vector.tensor_scalar_mul(out=dneg[:], in0=ident[:], scalar1=NEG_BIG)
+        nc.vector.tensor_scalar_mul(out=dneg[:], in0=ident[:], scalar1=BIG)
         warm = sbt([P, 2], F32, "warm")
         nc.vector.memset(warm[:, 0:1], 0.0)
         nc.scalar.activation(out=warm[:, 1:2], in_=warm[:, 0:1], func=ACT.Exp)
@@ -85,14 +92,13 @@ def tile_dynamicgraphattention_l_kernel(tc, H_t, A_stat, M_mask, Wq, Wk, out):
             else:
                 grp = wsrc[key[1]][CH * key[2]:CH * (key[2] + 1), :]
                 src = grp.rearrange("(m t) k -> m t k", t=4)[:, key[3], :]
-            early = key[0] == "w" or (key[1] == 0 and key[2] == 0)
-            t = sbt([P, KD], BF16, "big" if early else "hraw")
+            t = sbt([P, KD], BF16, "big" if key in early else "hraw")
             nc.sync.dma_start(out=t[:], in_=src)
             raw[key] = t
 
         def next_load(key):
-            q = pend_load[key[0]]
-            if q and key[0:3] != ("h", 0, 0):
+            q = pend_load["e" if key in early else "l"]
+            if q:
                 load_block(q.pop(0))
 
         def sort_block(key):
@@ -175,11 +181,11 @@ def tile_dynamicgraphattention_l_kernel(tc, H_t, A_stat, M_mask, Wq, Wk, out):
                     in_=g2t[:].rearrange("p n t -> p (n t)"),
                 )
 
-        def unit(b, c, w, G, slots):
+        def unit(n, b, c, w, G):
             tmp = sbt([P, 4, CH], BF16, "tmp")
             for t in range(4):
-                if t % 2 == 0 and slots:
-                    slots.pop(0)()
+                if t % 2 == 0 and (2 * n + t // 2) in run_at:
+                    do_run(run_at[2 * n + t // 2])
                 acc = pst([P, CH], "acc")
                 for g in range(NPASS):
                     nc.tensor.matmul_mx(
@@ -192,6 +198,9 @@ def tile_dynamicgraphattention_l_kernel(tc, H_t, A_stat, M_mask, Wq, Wk, out):
                         stop=(g == NPASS - 1),
                     )
                 nc.scalar.copy(out=tmp[:, t, :], in_=acc[:])
+                if t % 2 == 1:
+                    for key in sort_at.get(2 * n + t // 2, []):
+                        sort_block(key)
             g2t = sbt([P, CH, 4], BF16, "g2")
             nc.vector.tensor_copy(out=g2t[:], in_=tmp[:].rearrange("p t n -> p n t"))
             flush_q()
@@ -206,24 +215,27 @@ def tile_dynamicgraphattention_l_kernel(tc, H_t, A_stat, M_mask, Wq, Wk, out):
 
         def bias(i):
             a, m = amt[i]
-            nc.vector.tensor_scalar(out=m[:], in0=m[:], scalar1=0.0, scalar2=NEG_BIG, op0=ALU.is_le, op1=ALU.mult)
-            dg = a[:, P * i:P * (i + 1)]
+            nc.vector.tensor_scalar(out=m[:], in0=m[:], scalar1=0.0, scalar2=BIG, op0=ALU.is_le, op1=ALU.mult)
+            dg = m[:, P * i:P * (i + 1)]
             nc.vector.tensor_tensor(out=dg, in0=dg, in1=dneg[:], op=ALU.add)
-            if G_ADD:
-                nc.gpsimd.tensor_tensor(out=a[:], in0=a[:], in1=m[:], op=ALU.add)
-            else:
-                nc.vector.tensor_tensor(out=a[:], in0=a[:], in1=m[:], op=ALU.add)
+            nc.gpsimd.tensor_tensor(out=a[:], in0=m[:], in1=a[:], op=ALU.subtract)
 
         def exp_thunk(srow, nmx, sm):
             def f():
-                nc.scalar.activation(out=srow[:], in_=srow[:], func=ACT.Exp, bias=nmx[:], scale=1.0, accum_out=sm[:])
+                nc.scalar.activation(out=srow[:], in_=srow[:], func=ACT.Exp, bias=nmx[:], scale=-1.0, accum_out=sm[:])
             return f
 
         def norm_thunk(b, i, srow, sm):
             def f():
                 rs = sbt([P, 1], F32, "rs")
                 nc.vector.reciprocal(out=rs[:], in_=sm[:])
-                if b == 1 and i >= G_NORM_FROM:
+                if b == 1 and i == NRB - 1:
+                    hw = NT // 2
+                    nc.gpsimd.tensor_scalar(out=srow[:, hw:NT], in0=srow[:, hw:NT], scalar1=rs[:], scalar2=0.0, op0=ALU.mult, op1=ALU.add)
+                    nc.scalar.activation(out=srow[:, 0:hw], in_=srow[:, 0:hw], func=ACT.Copy, scale=rs[:])
+                    nc.scalar.dma_start(out=out[b, P * i:P * (i + 1), 0:hw], in_=srow[:, 0:hw])
+                    nc.sync.dma_start(out=out[b, P * i:P * (i + 1), hw:NT], in_=srow[:, hw:NT])
+                elif b == 1 and i >= G_NORM_FROM:
                     nc.gpsimd.tensor_scalar(out=srow[:], in0=srow[:], scalar1=rs[:], scalar2=0.0, op0=ALU.mult, op1=ALU.add)
                     nc.sync.dma_start(out=out[b, P * i:P * (i + 1), :], in_=srow[:])
                 else:
@@ -243,17 +255,19 @@ def tile_dynamicgraphattention_l_kernel(tc, H_t, A_stat, M_mask, Wq, Wk, out):
                 load_am(i + 2)
             tick()
             bm = amt[i][0]
+            for bb in ((0, 1) if (b == 0 and i <= MERGE_TP_UPTO) else ((b,) if (b == 0 or i > MERGE_TP_UPTO) else ())):
+                tpl = []
+                for q in range((i + 3) // 4):
+                    nblk = min(4, i - 4 * q)
+                    xt = pst([P, 4, P], "tp")
+                    for jj in range(nblk):
+                        blk = rt.pop((bb, 4 * q + jj, i))
+                        nc.tensor.transpose(xt[:, jj, :], blk, ident[:])
+                        rfree.append(blk)
+                    tpl.append((q, nblk, xt))
+                tps[bb] = tpl
             srow = sbt([P, NT], F32, "big")
-            tps = []
-            for q in range((i + 3) // 4):
-                nblk = min(4, i - 4 * q)
-                xt = pst([P, 4, P], "tp")
-                for jj in range(nblk):
-                    blk = rt.pop((b, 4 * q + jj, i))
-                    nc.tensor.transpose(xt[:, jj, :], blk, ident[:])
-                    rfree.append(blk)
-                tps.append((q, nblk, xt))
-            for q, nblk, xt in tps:
+            for q, nblk, xt in tps[b]:
                 nc.vector.tensor_tensor(
                     out=srow[:, CH * q:CH * q + P * nblk],
                     in0=xt[:, 0:nblk, :].rearrange("p j c -> p (j c)"),
@@ -285,7 +299,7 @@ def tile_dynamicgraphattention_l_kernel(tc, H_t, A_stat, M_mask, Wq, Wk, out):
                 wcols = (4 - lo) * P
                 col0 = CH * cj + P * lo
                 nc.vector.scalar_tensor_tensor(
-                    out=srow[:, col0:col0 + wcols], in0=acc[:, 0:wcols], scalar=LOGIT_SCALE,
+                    out=srow[:, col0:col0 + wcols], in0=acc[:, 0:wcols], scalar=-LOGIT_SCALE,
                     in1=bm[:, col0:col0 + wcols], op0=ALU.mult, op1=ALU.add,
                 )
                 for blk in range(lo, 4):
@@ -293,15 +307,13 @@ def tile_dynamicgraphattention_l_kernel(tc, H_t, A_stat, M_mask, Wq, Wk, out):
                     if j > i:
                         rtile = r_block()
                         nc.scalar.activation(
-                            out=rtile, in_=acc[:, (blk - lo) * P:(blk - lo + 1) * P], func=ACT.Copy, scale=LOGIT_SCALE
+                            out=rtile, in_=acc[:, (blk - lo) * P:(blk - lo + 1) * P], func=ACT.Copy, scale=-LOGIT_SCALE
                         )
                         rt[(b, i, j)] = rtile
                 if cj == ci:
                     tick()
-            mx = sbt([P, 1], F32, "mx")
-            nc.vector.reduce_max(out=mx[:], in_=srow[:], axis=AX.X)
             nmx = sbt([P, 1], F32, "nmx")
-            nc.vector.tensor_scalar_mul(out=nmx[:], in0=mx[:], scalar1=-1.0)
+            nc.vector.tensor_reduce(out=nmx[:], in_=srow[:], axis=AX.X, op=ALU.min)
             if b == (0 if G_ADD else 1) and i + 1 < NRB:
                 bias(i + 1)
             sm = sbt([P, 1], F32, "sm")
@@ -309,49 +321,61 @@ def tile_dynamicgraphattention_l_kernel(tc, H_t, A_stat, M_mask, Wq, Wk, out):
             later.append(norm_thunk(b, i, srow, sm))
 
         units = [(w, G) for w in range(2) for G in range(NPASS)]
-        wblocks = [("w", w, G, t) for w, G in units for t in range(4)]
-        head = [("h", 0, 0, 0), ("h", 0, 0, 1), wblocks[0], wblocks[1], ("h", 0, 0, 2), ("h", 0, 0, 3)] + wblocks[2:W_IN_FLIGHT]
-        for key in head:
+        order = []
+        preps = []
+        have_h = []
+        have_w = []
+        for kind, x in (("h", 0), ("w", 0), ("h", 1), ("w", 1), ("h", 2), ("w", 2), ("h", 3), ("w", 3), ("w", 4), ("w", 5), ("w", 6), ("w", 7)):
+            preps.append((kind, x, len(order)))
+            if kind == "h":
+                order.extend([(0, x, u) for u in have_w])
+                have_h.append(x)
+            else:
+                order.extend([(0, c, x) for c in have_h])
+                have_w.append(x)
+        for c in range(NCH):
+            preps.append(("h", NCH + c, len(order)))
+            order.extend([(1, c, u) for u in range(8)])
+
+        blocks = []
+        prologue = []
+        free_slot = 0
+        for kind, x, need in preps:
+            if kind == "h":
+                runs = hruns(x // NCH, x % NCH)
+            else:
+                runs = wruns(units[x][0], units[x][1])
+            blocks.extend(runs[0] + runs[1])
+            if need == 0:
+                prologue.append(runs)
+                continue
+            for rn in range(2):
+                s = max(2 * need - LEAD[rn], free_slot)
+                free_slot = s + 1
+                run_at[s] = runs[rn]
+                last = kind == "h" and x == 2 * NCH - 1
+                if s - SORT_LEAD >= SORT_FROM and not last:
+                    sort_at[s - SORT_LEAD] = runs[rn]
+        for key in blocks[0:N_EARLY]:
+            early.add(key)
+        for key in blocks[0:E_IN_FLIGHT]:
             load_block(key)
-        pend_load["w"].extend(wblocks[W_IN_FLIGHT:])
-        hq = [("h", m // NCH, m % NCH, r) for m in range(1, 2 * NCH) for r in range(4)]
-        load_block(hq[0])
-        load_block(hq[1])
-        pend_load["h"].extend(hq[2:])
+        pend_load["e"].extend(blocks[E_IN_FLIGHT:N_EARLY])
+        load_block(blocks[N_EARLY])
+        load_block(blocks[N_EARLY + 1])
+        pend_load["l"].extend(blocks[N_EARLY + 2:])
 
-        do_run(hruns(0, 0)[0][0:2])
-        do_run(wruns(0, 0)[0])
-        do_run(hruns(0, 0)[1])
-        do_run(wruns(0, 0)[1])
+        for runs in prologue:
+            for rn in range(2):
+                do_run(runs[rn])
 
-        for m in range(2 * NCH):
-            nruns = hruns((m + 1) // NCH, (m + 1) % NCH) if m + 1 < 2 * NCH else []
-            do_sort = SORT_H and m < 2 * NCH - 2
-            for ui in range(8):
-                w, G = units[ui]
-                slots = []
-                if m == 0 and ui < 7:
-                    slots = [run_thunk(k) for k in wruns(units[ui + 1][0], units[ui + 1][1])]
-                elif nruns and m == 0 and ui == 7:
-                    slots = [run_thunk(k) for k in nruns]
-                elif nruns and m > 0 and ui == 4:
-                    slots = [run_thunk(nruns[0])]
-                elif nruns and m > 0 and ui == 6:
-                    slots = [run_thunk(nruns[1])]
-                unit(m // NCH, m % NCH, w, G, slots)
-                if do_sort and ui == (5 if m == 0 else 2):
-                    sort_block(nruns[0][0])
-                    sort_block(nruns[0][1])
-                if do_sort and ui == (6 if m == 0 else 4):
-                    sort_block(nruns[1][0])
-                    sort_block(nruns[1][1])
-                if m == 0 and ui < 6 and SORT_W:
-                    for k in wruns(units[ui + 2][0], units[ui + 2][1])[0][0:SORT_W]:
-                        sort_block(k)
-                if m == 2 * NCH - 1 and ui == 3:
-                    load_am(0)
-                if m == 2 * NCH - 1 and ui == 6:
-                    bias(0)
+        for n in range(len(order)):
+            b, c, u = order[n]
+            unit(n, b, c, units[u][0], units[u][1])
+            if n == len(order) - 5:
+                load_am(0)
+            if n == len(order) - 2:
+                bias(0)
         flush_q()
         load_am(1)
 

@@ -32,11 +32,8 @@ BUFS = {
 }
 LEAD = (7, 3)
 SORT_LEAD = 3
-SORT_FROM = 3
 N_EARLY = 28
 E_IN_FLIGHT = 8
-G_ADD = True
-G_NORM_FROM = 6
 MERGE_TP_UPTO = 8
 
 
@@ -103,7 +100,11 @@ def tile_dynamicgraphattention_l_kernel(tc, H_t, A_stat, M_mask, Wq, Wk, out):
 
         def sort_block(key):
             s = sbt([P, NPASS, 2, P], F32, "big")
-            nc.scalar.copy(out=s[:], in_=raw[key][:].bitcast(F32).rearrange("r (g p u) -> r g u p", g=NPASS, u=2))
+            src = raw[key][:].bitcast(F32).rearrange("r (g p u) -> r g u p", g=NPASS, u=2)
+            if key in early and key[3] % 2 == 1:
+                nc.vector.tensor_copy(out=s[:], in_=src)
+            else:
+                nc.scalar.copy(out=s[:], in_=src)
             srt[key] = s
             next_load(key)
 
@@ -213,9 +214,12 @@ def tile_dynamicgraphattention_l_kernel(tc, H_t, A_stat, M_mask, Wq, Wk, out):
             nc.sync.dma_start(out=m[:], in_=M_mask[P * i:P * (i + 1), :])
             amt[i] = (a, m)
 
-        def bias(i):
-            a, m = amt[i]
+        def bias_mask(i):
+            m = amt[i][1]
             nc.vector.tensor_scalar(out=m[:], in0=m[:], scalar1=0.0, scalar2=BIG, op0=ALU.is_le, op1=ALU.mult)
+
+        def bias_sum(i):
+            a, m = amt[i]
             dg = m[:, P * i:P * (i + 1)]
             nc.vector.tensor_tensor(out=dg, in0=dg, in1=dneg[:], op=ALU.add)
             nc.gpsimd.tensor_tensor(out=a[:], in0=m[:], in1=a[:], op=ALU.subtract)
@@ -235,9 +239,6 @@ def tile_dynamicgraphattention_l_kernel(tc, H_t, A_stat, M_mask, Wq, Wk, out):
                     nc.scalar.activation(out=srow[:, 0:hw], in_=srow[:, 0:hw], func=ACT.Copy, scale=rs[:])
                     nc.scalar.dma_start(out=out[b, P * i:P * (i + 1), 0:hw], in_=srow[:, 0:hw])
                     nc.sync.dma_start(out=out[b, P * i:P * (i + 1), hw:NT], in_=srow[:, hw:NT])
-                elif b == 1 and i >= G_NORM_FROM:
-                    nc.gpsimd.tensor_scalar(out=srow[:], in0=srow[:], scalar1=rs[:], scalar2=0.0, op0=ALU.mult, op1=ALU.add)
-                    nc.sync.dma_start(out=out[b, P * i:P * (i + 1), :], in_=srow[:])
                 else:
                     nc.scalar.activation(out=srow[:], in_=srow[:], func=ACT.Copy, scale=rs[:])
                     nc.scalar.dma_start(out=out[b, P * i:P * (i + 1), :], in_=srow[:])
@@ -312,10 +313,12 @@ def tile_dynamicgraphattention_l_kernel(tc, H_t, A_stat, M_mask, Wq, Wk, out):
                         rt[(b, i, j)] = rtile
                 if cj == ci:
                     tick()
+            if b == 0 and i + 1 < NRB:
+                bias_mask(i + 1)
             nmx = sbt([P, 1], F32, "nmx")
             nc.vector.tensor_reduce(out=nmx[:], in_=srow[:], axis=AX.X, op=ALU.min)
-            if b == (0 if G_ADD else 1) and i + 1 < NRB:
-                bias(i + 1)
+            if b == 0 and i + 1 < NRB:
+                bias_sum(i + 1)
             sm = sbt([P, 1], F32, "sm")
             later.append(exp_thunk(srow, nmx, sm))
             later.append(norm_thunk(b, i, srow, sm))
@@ -354,8 +357,9 @@ def tile_dynamicgraphattention_l_kernel(tc, H_t, A_stat, M_mask, Wq, Wk, out):
                 free_slot = s + 1
                 run_at[s] = runs[rn]
                 last = kind == "h" and x == 2 * NCH - 1
-                if s - SORT_LEAD >= SORT_FROM and not last:
-                    sort_at[s - SORT_LEAD] = runs[rn]
+                if not last:
+                    sp = max(s - SORT_LEAD, -1)
+                    sort_at[sp] = sort_at.get(sp, []) + runs[rn]
         for key in blocks[0:N_EARLY]:
             early.add(key)
         for key in blocks[0:E_IN_FLIGHT]:
@@ -369,13 +373,17 @@ def tile_dynamicgraphattention_l_kernel(tc, H_t, A_stat, M_mask, Wq, Wk, out):
             for rn in range(2):
                 do_run(runs[rn])
 
+        for key in sort_at.get(-1, []):
+            sort_block(key)
+
         for n in range(len(order)):
             b, c, u = order[n]
             unit(n, b, c, units[u][0], units[u][1])
             if n == len(order) - 5:
                 load_am(0)
             if n == len(order) - 2:
-                bias(0)
+                bias_mask(0)
+                bias_sum(0)
         flush_q()
         load_am(1)
 

@@ -32,9 +32,13 @@ BUFS = {
 }
 LEAD = (7, 3)
 SORT_LEAD = 3
+SORT_FROM = 3
 N_EARLY = 28
 E_IN_FLIGHT = 8
-MERGE_TP_UPTO = 8
+G_ADD = True
+G_NORM_FROM = 6
+MERGE_TP_UPTO = 6
+LATE_AT = 4
 
 
 def tile_dynamicgraphattention_l_kernel(tc, H_t, A_stat, M_mask, Wq, Wk, out):
@@ -100,11 +104,7 @@ def tile_dynamicgraphattention_l_kernel(tc, H_t, A_stat, M_mask, Wq, Wk, out):
 
         def sort_block(key):
             s = sbt([P, NPASS, 2, P], F32, "big")
-            src = raw[key][:].bitcast(F32).rearrange("r (g p u) -> r g u p", g=NPASS, u=2)
-            if key in early and key[3] % 2 == 1:
-                nc.vector.tensor_copy(out=s[:], in_=src)
-            else:
-                nc.scalar.copy(out=s[:], in_=src)
+            nc.scalar.copy(out=s[:], in_=raw[key][:].bitcast(F32).rearrange("r (g p u) -> r g u p", g=NPASS, u=2))
             srt[key] = s
             next_load(key)
 
@@ -214,12 +214,9 @@ def tile_dynamicgraphattention_l_kernel(tc, H_t, A_stat, M_mask, Wq, Wk, out):
             nc.sync.dma_start(out=m[:], in_=M_mask[P * i:P * (i + 1), :])
             amt[i] = (a, m)
 
-        def bias_mask(i):
-            m = amt[i][1]
-            nc.vector.tensor_scalar(out=m[:], in0=m[:], scalar1=0.0, scalar2=BIG, op0=ALU.is_le, op1=ALU.mult)
-
-        def bias_sum(i):
+        def bias(i):
             a, m = amt[i]
+            nc.vector.tensor_scalar(out=m[:], in0=m[:], scalar1=0.0, scalar2=BIG, op0=ALU.is_le, op1=ALU.mult)
             dg = m[:, P * i:P * (i + 1)]
             nc.vector.tensor_tensor(out=dg, in0=dg, in1=dneg[:], op=ALU.add)
             nc.gpsimd.tensor_tensor(out=a[:], in0=m[:], in1=a[:], op=ALU.subtract)
@@ -239,6 +236,9 @@ def tile_dynamicgraphattention_l_kernel(tc, H_t, A_stat, M_mask, Wq, Wk, out):
                     nc.scalar.activation(out=srow[:, 0:hw], in_=srow[:, 0:hw], func=ACT.Copy, scale=rs[:])
                     nc.scalar.dma_start(out=out[b, P * i:P * (i + 1), 0:hw], in_=srow[:, 0:hw])
                     nc.sync.dma_start(out=out[b, P * i:P * (i + 1), hw:NT], in_=srow[:, hw:NT])
+                elif b == 1 and i >= G_NORM_FROM:
+                    nc.gpsimd.tensor_scalar(out=srow[:], in0=srow[:], scalar1=rs[:], scalar2=0.0, op0=ALU.mult, op1=ALU.add)
+                    nc.sync.dma_start(out=out[b, P * i:P * (i + 1), :], in_=srow[:])
                 else:
                     nc.scalar.activation(out=srow[:], in_=srow[:], func=ACT.Copy, scale=rs[:])
                     nc.scalar.dma_start(out=out[b, P * i:P * (i + 1), :], in_=srow[:])
@@ -311,14 +311,12 @@ def tile_dynamicgraphattention_l_kernel(tc, H_t, A_stat, M_mask, Wq, Wk, out):
                             out=rtile, in_=acc[:, (blk - lo) * P:(blk - lo + 1) * P], func=ACT.Copy, scale=-LOGIT_SCALE
                         )
                         rt[(b, i, j)] = rtile
-                if cj == ci:
+                if cj == NCH - 1:
                     tick()
-            if b == 0 and i + 1 < NRB:
-                bias_mask(i + 1)
             nmx = sbt([P, 1], F32, "nmx")
             nc.vector.tensor_reduce(out=nmx[:], in_=srow[:], axis=AX.X, op=ALU.min)
-            if b == 0 and i + 1 < NRB:
-                bias_sum(i + 1)
+            if b == (0 if G_ADD else 1) and i + 1 < NRB:
+                bias(i + 1)
             sm = sbt([P, 1], F32, "sm")
             later.append(exp_thunk(srow, nmx, sm))
             later.append(norm_thunk(b, i, srow, sm))
@@ -357,33 +355,29 @@ def tile_dynamicgraphattention_l_kernel(tc, H_t, A_stat, M_mask, Wq, Wk, out):
                 free_slot = s + 1
                 run_at[s] = runs[rn]
                 last = kind == "h" and x == 2 * NCH - 1
-                if not last:
-                    sp = max(s - SORT_LEAD, -1)
-                    sort_at[sp] = sort_at.get(sp, []) + runs[rn]
+                if s - SORT_LEAD >= SORT_FROM and not last:
+                    sort_at[s - SORT_LEAD] = runs[rn]
         for key in blocks[0:N_EARLY]:
             early.add(key)
         for key in blocks[0:E_IN_FLIGHT]:
             load_block(key)
         pend_load["e"].extend(blocks[E_IN_FLIGHT:N_EARLY])
-        load_block(blocks[N_EARLY])
-        load_block(blocks[N_EARLY + 1])
-        pend_load["l"].extend(blocks[N_EARLY + 2:])
+        pend_load["l"].extend(blocks[N_EARLY:])
 
         for runs in prologue:
             for rn in range(2):
                 do_run(runs[rn])
 
-        for key in sort_at.get(-1, []):
-            sort_block(key)
-
         for n in range(len(order)):
             b, c, u = order[n]
             unit(n, b, c, units[u][0], units[u][1])
+            if n == LATE_AT:
+                load_block(pend_load["l"].pop(0))
+                load_block(pend_load["l"].pop(0))
             if n == len(order) - 5:
                 load_am(0)
             if n == len(order) - 2:
-                bias_mask(0)
-                bias_sum(0)
+                bias(0)
         flush_q()
         load_am(1)
 

from contextlib import ExitStack
import math

import concourse.mybir as mybir
from concourse.masks import make_identity

F32 = mybir.dt.float32
BF16 = mybir.dt.bfloat16
U32 = mybir.dt.uint32
U8 = mybir.dt.uint8
FP8X4 = mybir.dt.float8_e4m3fn_x4
ACT = mybir.ActivationFunctionType
ALU = mybir.AluOpType
AX = mybir.AxisListType

P = 128
NT = 2048
KD = 2048
CH = 512
NPASS = KD // CH
NCH = NT // CH
NRB = NT // P
FLOPS = 3 * 2 * 2 * 2048 * 2048 * 2048
LOGIT_SCALE = 0.5 / (math.sqrt(2048.0) * 1.5)
BIG = 1.0e30

BUFS = {
    "ident": 1, "dneg": 1, "warm": 1,
    "big": 24, "pl": 24,
    "hraw": 2, "gin": 3, "g2": 2, "tmp": 2,
    "nmx": 3, "sm": 3, "rs": 3,
}
LEAD = (7, 3)
SORT_LEAD = 3
SORT_FROM = 3
N_EARLY = 28
E_IN_FLIGHT = 8
G_ADD = True
G_NORM_FROM = 6
MERGE_TP_UPTO = 6
LATE_AT = 4


def tile_dynamicgraphattention_l_kernel(tc, H_t, A_stat, M_mask, Wq, Wk, out):
    nc = tc.nc
    with ExitStack() as ctx:
        sb = ctx.enter_context(tc.tile_pool(name="sb", bufs=1))
        ps = ctx.enter_context(tc.psum_pool(name="ps", bufs=4))
        ctx.enter_context(tc.manual_schedule())

        def sbt(shape, dtype, tag):
            return sb.tile(shape, dtype, name="t_%s" % tag, tag=tag, bufs=BUFS[tag], align_bytes=64)

        def pst(shape, tag):
            return ps.tile(shape, F32, name="p_%s" % tag, tag=tag, bufs=4)

        wsrc = (Wq, Wk)
        wc = {}
        wp = {}
        hc = {}
        hp = {}
        qk = {}
        qkp = {}
        raw = {}
        srt = {}
        rt = {}
        amt = {}
        pend_load = {"e": [], "l": []}
        early = set()
        run_at = {}
        sort_at = {}
        pendq = []
        later = []
        rfree = []
        tps = {}

        ident = sbt([P, P], F32, "ident")
        make_identity(nc, ident[:])
        dneg = sbt([P, P], BF16, "dneg")
        nc.vector.tensor_scalar_mul(out=dneg[:], in0=ident[:], scalar1=BIG)
        warm = sbt([P, 2], F32, "warm")
        nc.vector.memset(warm[:, 0:1], 0.0)
        nc.scalar.activation(out=warm[:, 1:2], in_=warm[:, 0:1], func=ACT.Exp)

        def tick():
            if later:
                later.pop(0)()

        def load_block(key):
            if key[0] == "h":
                row0 = CH * key[2] + P * key[3]
                src = H_t[key[1], row0:row0 + P, :]
            else:
                grp = wsrc[key[1]][CH * key[2]:CH * (key[2] + 1), :]
                src = grp.rearrange("(m t) k -> m t k", t=4)[:, key[3], :]
            t = sbt([P, KD], BF16, "big" if key in early else "hraw")
            nc.sync.dma_start(out=t[:], in_=src)
            raw[key] = t

        def next_load(key):
            q = pend_load["e" if key in early else "l"]
            if q:
                load_block(q.pop(0))

        def sort_block(key):
            s = sbt([P, NPASS, 2, P], F32, "big")
            nc.scalar.copy(out=s[:], in_=raw[key][:].bitcast(F32).rearrange("r (g p u) -> r g u p", g=NPASS, u=2))
            srt[key] = s
            next_load(key)

        def block_dest(key):
            kk = (key[1], key[2])
            cd, pl = (hc, hp) if key[0] == "h" else (wc, wp)
            if kk not in cd:
                cd[kk] = sbt([P, NPASS, CH], U32, "big")
                pl[kk] = sbt([P, CH], U8, "pl")
            return cd[kk], pl[kk]

        def quant_bank(item):
            key, h, gin = item
            codes, planes = block_dest(key)
            col = P * key[3]
            for g2 in range(2):
                g = 2 * h + g2
                nc.vector.quantize_mx(
                    out=codes[:, g, col:col + P].bitcast(FP8X4),
                    scales=planes[4 * g:P, col:col + P],
                    in_=gin[:, g2].rearrange("p r j -> p (r j)"),
                )

        def do_run(keys):
            banks = []
            for key in keys:
                words = raw[key][:].bitcast(F32)
                for h in range(2):
                    xt = pst([P, 2, 2, P], "tp")
                    for g2 in range(2):
                        g = 2 * h + g2
                        for u in range(2):
                            if key in srt:
                                nc.tensor.transpose(xt[:, g2, u, :], srt[key][:, g, u, :], ident[:])
                            else:
                                nc.tensor.transpose(xt[:, g2, u, :], words[:, 256 * g + u:256 * (g + 1):2], ident[:])
                    banks.append((key, h, xt))
                if key not in srt:
                    next_load(key)
            gins = []
            for n in range(len(banks)):
                key, h, xt = banks[n]
                if n == 3:
                    quant_bank(gins[0])
                gin = sbt([P, 2, P, 4], BF16, "gin")
                src = xt[:].rearrange("p g u r -> p g r u")
                if n % 2 == 0:
                    nc.scalar.copy(out=gin[:].bitcast(F32), in_=src)
                else:
                    nc.vector.tensor_copy(out=gin[:].bitcast(F32), in_=src)
                gins.append((key, h, gin))
            for n in range(1, len(gins)):
                quant_bank(gins[n])

        def run_thunk(keys):
            def f():
                do_run(keys)
            return f

        def hruns(b, c):
            return [[("h", b, c, 0), ("h", b, c, 1)], [("h", b, c, 2), ("h", b, c, 3)]]

        def wruns(w, G):
            return [[("w", w, G, 0), ("w", w, G, 1)], [("w", w, G, 2), ("w", w, G, 3)]]

        def flush_q():
            while pendq:
                g2t, kk, G = pendq.pop(0)
                if kk not in qk:
                    qk[kk] = sbt([P, NPASS, CH], U32, "big")
                    qkp[kk] = sbt([P, CH], U8, "pl")
                nc.vector.quantize_mx(
                    out=qk[kk][:, G, :].bitcast(FP8X4),
                    scales=qkp[kk][4 * G:P, :],
                    in_=g2t[:].rearrange("p n t -> p (n t)"),
                )

        def unit(n, b, c, w, G):
            tmp = sbt([P, 4, CH], BF16, "tmp")
            for t in range(4):
                if t % 2 == 0 and (2 * n + t // 2) in run_at:
                    do_run(run_at[2 * n + t // 2])
                acc = pst([P, CH], "acc")
                for g in range(NPASS):
                    nc.tensor.matmul_mx(
                        out=acc[:],
                        lhsT=wc[(w, G)][:, g, P * t:P * (t + 1)].bitcast(FP8X4),
                        lhsT_scale=wp[(w, G)][4 * g:P, P * t:P * (t + 1)],
                        rhs=hc[(b, c)][:, g, :].bitcast(FP8X4),
                        rhs_scale=hp[(b, c)][4 * g:P, :],
                        start=(g == 0),
                        stop=(g == NPASS - 1),
                    )
                nc.scalar.copy(out=tmp[:, t, :], in_=acc[:])
                if t % 2 == 1:
                    for key in sort_at.get(2 * n + t // 2, []):
                        sort_block(key)
            g2t = sbt([P, CH, 4], BF16, "g2")
            nc.vector.tensor_copy(out=g2t[:], in_=tmp[:].rearrange("p t n -> p n t"))
            flush_q()
            pendq.append((g2t, (b, w, c), G))

        def load_am(i):
            a = sbt([P, NT], BF16, "hraw" if i % 2 == 0 else "g2")
            nc.sync.dma_start(out=a[:], in_=A_stat[P * i:P * (i + 1), :])
            m = sbt([P, NT], BF16, "hraw" if i == 0 else "tmp")
            nc.sync.dma_start(out=m[:], in_=M_mask[P * i:P * (i + 1), :])
            amt[i] = (a, m)

        def bias(i):
            a, m = amt[i]
            nc.vector.tensor_scalar(out=m[:], in0=m[:], scalar1=0.0, scalar2=BIG, op0=ALU.is_le, op1=ALU.mult)
            dg = m[:, P * i:P * (i + 1)]
            nc.vector.tensor_tensor(out=dg, in0=dg, in1=dneg[:], op=ALU.add)
            nc.gpsimd.tensor_tensor(out=a[:], in0=m[:], in1=a[:], op=ALU.subtract)

        def exp_thunk(srow, nmx, sm):
            def f():
                nc.scalar.activation(out=srow[:], in_=srow[:], func=ACT.Exp, bias=nmx[:], scale=-1.0, accum_out=sm[:])
            return f

        def norm_thunk(b, i, srow, sm):
            def f():
                rs = sbt([P, 1], F32, "rs")
                nc.vector.reciprocal(out=rs[:], in_=sm[:])
                if b == 1 and i == NRB - 1:
                    hw = NT // 2
                    nc.gpsimd.tensor_scalar(out=srow[:, hw:NT], in0=srow[:, hw:NT], scalar1=rs[:], scalar2=0.0, op0=ALU.mult, op1=ALU.add)
                    nc.scalar.activation(out=srow[:, 0:hw], in_=srow[:, 0:hw], func=ACT.Copy, scale=rs[:])
                    nc.scalar.dma_start(out=out[b, P * i:P * (i + 1), 0:hw], in_=srow[:, 0:hw])
                    nc.sync.dma_start(out=out[b, P * i:P * (i + 1), hw:NT], in_=srow[:, hw:NT])
                elif b == 1 and i >= G_NORM_FROM:
                    nc.gpsimd.tensor_scalar(out=srow[:], in0=srow[:], scalar1=rs[:], scalar2=0.0, op0=ALU.mult, op1=ALU.add)
                    nc.sync.dma_start(out=out[b, P * i:P * (i + 1), :], in_=srow[:])
                else:
                    nc.scalar.activation(out=srow[:], in_=srow[:], func=ACT.Copy, scale=rs[:])
                    nc.scalar.dma_start(out=out[b, P * i:P * (i + 1), :], in_=srow[:])
            return f

        def r_block():
            if not rfree:
                page = sbt([P, 16, P], F32, "big")
                for n in range(16):
                    rfree.append(page[:, n, :])
            return rfree.pop(0)

        def row_step(b, i):
            if b == 1 and i + 2 < NRB:
                load_am(i + 2)
            tick()
            bm = amt[i][0]
            for bb in ((0, 1) if (b == 0 and i <= MERGE_TP_UPTO) else ((b,) if (b == 0 or i > MERGE_TP_UPTO) else ())):
                tpl = []
                for q in range((i + 3) // 4):
                    nblk = min(4, i - 4 * q)
                    xt = pst([P, 4, P], "tp")
                    for jj in range(nblk):
                        blk = rt.pop((bb, 4 * q + jj, i))
                        nc.tensor.transpose(xt[:, jj, :], blk, ident[:])
                        rfree.append(blk)
                    tpl.append((q, nblk, xt))
                tps[bb] = tpl
            srow = sbt([P, NT], F32, "big")
            for q, nblk, xt in tps[b]:
                nc.vector.tensor_tensor(
                    out=srow[:, CH * q:CH * q + P * nblk],
                    in0=xt[:, 0:nblk, :].rearrange("p j c -> p (j c)"),
                    in1=bm[:, CH * q:CH * q + P * nblk],
                    op=ALU.add,
                )
            ci, r = divmod(i, 4)
            for cj in range(ci, NCH):
                lo = r if cj == ci else 0
                groups = {0: [(0, 4)], 1: [(1, 1), (2, 2)], 2: [(2, 2)], 3: [(3, 1)]}[lo]
                acc = pst([P, CH], "acc")
                for b0, nb in groups:
                    o0 = (b0 - lo) * P
                    n = 0
                    for G in range(NPASS):
                        for sa in range(2):
                            st = (b, sa, ci)
                            mv = (b, 1 - sa, cj)
                            nc.tensor.matmul_mx(
                                out=acc[:, o0:o0 + P * nb],
                                lhsT=qk[st][:, G, P * r:P * (r + 1)].bitcast(FP8X4),
                                lhsT_scale=qkp[st][4 * G:P, P * r:P * (r + 1)],
                                rhs=qk[mv][:, G, P * b0:P * (b0 + nb)].bitcast(FP8X4),
                                rhs_scale=qkp[mv][4 * G:P, P * b0:P * (b0 + nb)],
                                start=(n == 0),
                                stop=(n == 2 * NPASS - 1),
                            )
                            n += 1
                wcols = (4 - lo) * P
                col0 = CH * cj + P * lo
                nc.vector.scalar_tensor_tensor(
                    out=srow[:, col0:col0 + wcols], in0=acc[:, 0:wcols], scalar=-LOGIT_SCALE,
                    in1=bm[:, col0:col0 + wcols], op0=ALU.mult, op1=ALU.add,
                )
                for blk in range(lo, 4):
                    j = 4 * cj + blk
                    if j > i:
                        rtile = r_block()
                        nc.scalar.activation(
                            out=rtile, in_=acc[:, (blk - lo) * P:(blk - lo + 1) * P], func=ACT.Copy, scale=-LOGIT_SCALE
                        )
                        rt[(b, i, j)] = rtile
                if cj == NCH - 1:
                    tick()
            nmx = sbt([P, 1], F32, "nmx")
            nc.vector.tensor_reduce(out=nmx[:], in_=srow[:], axis=AX.X, op=ALU.min)
            if b == (0 if G_ADD else 1) and i + 1 < NRB:
                bias(i + 1)
            sm = sbt([P, 1], F32, "sm")
            later.append(exp_thunk(srow, nmx, sm))
            later.append(norm_thunk(b, i, srow, sm))

        units = [(w, G) for w in range(2) for G in range(NPASS)]
        order = []
        preps = []
        have_h = []
        have_w = []
        for kind, x in (("h", 0), ("w", 0), ("h", 1), ("w", 1), ("h", 2), ("w", 2), ("h", 3), ("w", 3), ("w", 4), ("w", 5), ("w", 6), ("w", 7)):
            preps.append((kind, x, len(order)))
            if kind == "h":
                order.extend([(0, x, u) for u in have_w])
                have_h.append(x)
            else:
                order.extend([(0, c, x) for c in have_h])
                have_w.append(x)
        for c in range(NCH):
            preps.append(("h", NCH + c, len(order)))
            order.extend([(1, c, u) for u in range(8)])

        blocks = []
        prologue = []
        free_slot = 0
        for kind, x, need in preps:
            if kind == "h":
                runs = hruns(x // NCH, x % NCH)
            else:
                runs = wruns(units[x][0], units[x][1])
            blocks.extend(runs[0] + runs[1])
            if need == 0:
                prologue.append(runs)
                continue
            for rn in range(2):
                s = max(2 * need - LEAD[rn], free_slot)
                free_slot = s + 1
                run_at[s] = runs[rn]
                last = kind == "h" and x == 2 * NCH - 1
                if s - SORT_LEAD >= SORT_FROM and not last:
                    sort_at[s - SORT_LEAD] = runs[rn]
        for key in blocks[0:N_EARLY]:
            early.add(key)
        for key in blocks[0:E_IN_FLIGHT]:
            load_block(key)
        pend_load["e"].extend(blocks[E_IN_FLIGHT:N_EARLY])
        pend_load["l"].extend(blocks[N_EARLY:])

        for runs in prologue:
            for rn in range(2):
                do_run(runs[rn])

        for n in range(len(order)):
            b, c, u = order[n]
            unit(n, b, c, units[u][0], units[u][1])
            if n == LATE_AT:
                load_block(pend_load["l"].pop(0))
                load_block(pend_load["l"].pop(0))
            if n == len(order) - 5:
                load_am(0)
            if n == len(order) - 2:
                bias(0)
        flush_q()
        load_am(1)

        for i in range(NRB):
            for b in range(2):
                row_step(b, i)
        while later:
            tick()
